import numpy as np
import ml_dtypes


def mxq(x, axis, fmt="e4m3"):
    dtype, down = {"e4m3": (ml_dtypes.float8_e4m3fn, 7), "e5m2": (ml_dtypes.float8_e5m2, 14)}[fmt]
    v = np.moveaxis(np.asarray(x, np.float32).astype(ml_dtypes.bfloat16).astype(np.float64), axis, -1)
    blocks = v.reshape(v.shape[:-1] + (-1, 32))
    amax = np.abs(blocks).max(-1, keepdims=True)
    byte = np.maximum(np.where(amax > 0, np.frexp(amax)[1] - 1 + 127, 0) - down, 1)
    scale = np.exp2(byte - 127.0)
    codes = (blocks / scale).astype(np.float32).astype(dtype).astype(np.float64)
    return np.moveaxis((codes * scale).reshape(v.shape), -1, axis)


WIDE = False


def mx_kscale(k):
    if not WIDE:
        return np.ones(k)
    levels = np.array([30, -30])
    if k % 512:
        return np.exp2(np.random.permutation(np.resize(levels, k // 32))).repeat(32)
    a = np.empty((k // 512, 16))
    for p in range(k // 512):
        a[p, :8] = np.random.permutation(np.resize(levels, 8))
        for g in range(8):
            far = levels[np.abs(levels - a[p, g]) >= 10]
            a[p, g + 8] = far[np.random.randint(len(far))]
    return np.exp2(a.ravel()).repeat(32)


BF16 = ml_dtypes.bfloat16


def bf(x):
    return np.asarray(x, np.float32).astype(BF16)


def f64(x):
    return np.asarray(x).astype(np.float64)


E2M1 = np.array([0.0, 0.5, 1.0, 1.5, 2.0, 3.0, 4.0, 6.0, -0.0, -0.5, -1.0, -1.5, -2.0, -3.0, -4.0, -6.0])


def pack_weight(w, fmt):
    k, n = w.shape
    w = f64(bf(w)).reshape(k // 32, 32, n)
    amax = np.abs(w).max(1)
    if fmt == "e4m3":
        byte = np.frexp(amax)[1] - 1 + 127 - 7
    else:
        mant, ex = np.frexp(amax / 6.0)
        byte = np.where(mant > 0.5, ex, ex - 1) + 127
    byte = np.clip(np.where(amax > 0, byte, 1), 1, 254)
    scaled = (w * np.exp2(127.0 - byte)[:, None, :]).reshape(k, n).astype(np.float32)
    by_word = np.ascontiguousarray(scaled.reshape(k // 512, 128, 4, n).transpose(0, 1, 3, 2))
    if fmt == "e4m3":
        words = by_word.astype(ml_dtypes.float8_e4m3fn).view(np.uint8)
    else:
        c = by_word.astype(ml_dtypes.float4_e2m1fn).view(np.uint8) & 0xF
        words = c[..., 0::2] | (c[..., 1::2] << 4)
    return np.ascontiguousarray(words), np.ascontiguousarray(byte.astype(np.uint8).reshape(k // 512, 16, n))


def unpack_weight(words, scales, fmt):
    g, p, n, _ = words.shape
    if fmt == "e4m3":
        vals = np.ascontiguousarray(words).view(ml_dtypes.float8_e4m3fn).astype(np.float64)
    else:
        nib = np.empty((g, p, n, 4), np.uint8)
        nib[..., 0::2] = words & 0xF
        nib[..., 1::2] = words >> 4
        vals = E2M1[nib]
    vals = vals * np.repeat(np.exp2(scales.astype(np.float64) - 127.0), 8, axis=1)[..., None]
    return vals.transpose(0, 1, 3, 2).reshape(g * 512, n)

def pack4(w):
    words, scales = pack_weight(w, "e2m1")
    return words.reshape(words.shape[0], 128, -1), scales


def unpack4(words, scales):
    return unpack_weight(words.reshape(words.shape[0], 128, -1, 2), scales, "e2m1")


B, N, DIM, H, DH = 2, 256, 1536, 16, 96
D1 = DH // 3


def rotate_half(t):
    d = t.shape[-1]
    t1, t2 = t[..., : (d + 1) // 2], t[..., (d + 1) // 2:]
    return np.concatenate((-t2, t1), axis=-1)


def apply_rope(t, freqs):
    return t * np.cos(freqs) + rotate_half(t) * np.sin(freqs)


def rope3(t, fs):
    return np.concatenate([apply_rope(ts, f) for ts, f in zip(np.split(t, (D1, 2 * D1), axis=-1), fs)], axis=-1)


def setup_inputs():
    s = mx_kscale(DIM)
    x = bf(np.random.standard_normal((B, N, DIM)) * s)
    f1 = bf(np.random.uniform(0.0, 1.0, (N, D1)))
    f2 = bf(np.random.uniform(0.0, 1.0, (N, D1)))
    f3 = bf(np.random.uniform(0.0, 1.0, (N, D1)))
    words, scales = pack4(np.random.standard_normal((DIM, 3 * H * DH)) / np.sqrt(DIM) / s[:, None])
    return {"x": x, "f1": f1, "f2": f2, "f3": f3, "Wqkv_words": words, "Wqkv_scales": scales}


def reference(x, f1, f2, f3, Wqkv_words, Wqkv_scales):
    qkv = mxq(f64(x), 2, "e5m2") @ unpack4(Wqkv_words, Wqkv_scales)
    q, k, v = np.split(qkv, 3, axis=-1)
    to_heads = lambda t: t.reshape(B, N, H, DH).transpose(0, 2, 1, 3)
    q, k, v = to_heads(q), to_heads(k), to_heads(v)
    fs = (f64(f1), f64(f2), f64(f3))
    return rope3(q, fs), rope3(k, fs), v

@@ -1,0 +1,242 @@
+import math
+from contextlib import ExitStack
+
+import concourse.mybir as mybir
+from concourse.masks import make_identity
+
+B, N, DIM, H, DH = 2, 256, 1536, 16, 96
+FLOPS = 2 * B * N * DIM * 3 * H * DH
+
+F32 = mybir.dt.float32
+BF16 = mybir.dt.bfloat16
+I32 = mybir.dt.int32
+U32 = mybir.dt.uint32
+U8 = mybir.dt.uint8
+E5M2X4 = mybir.dt.float8_e5m2_x4
+E2M1X4 = mybir.dt.float4_e2m1fn_x4
+MULT = mybir.AluOpType.mult
+ADD = mybir.AluOpType.add
+SIN = mybir.ActivationFunctionType.Sin
+
+P = 128
+PASSES = DIM // 512
+TILES = 4
+WIDTH = H * DH
+GROUP = 32
+HALF = GROUP // 2
+ROPE_HEADS = 4
+ROPE_COLS = ROPE_HEADS * DH
+ROPE_BLOCKS = 2 * H // ROPE_HEADS
+V_BLOCKS = ((0, 512), (512, 1024), (1024, 1280), (1280, 1536))
+V_STORES = ((0, 5), (5, 10), (10, 13), (13, 16))
+W_CHUNKS = ((0, ROPE_COLS), (ROPE_COLS, WIDTH), (2 * WIDTH, 3 * WIDTH), (WIDTH, 2 * WIDTH))
+S_CHUNKS = ((0, 2 * ROPE_COLS), (2 * ROPE_COLS, 3 * WIDTH))
+
+
+def tile_attention_pa_kernel(tc, x, f1, f2, f3, w_words, w_scales, out_q, out_k, out_v):
+    nc = tc.nc
+    with ExitStack() as ctx:
+        keep = ctx.enter_context(tc.tile_pool(name="keep", bufs=1))
+        stage = ctx.enter_context(tc.tile_pool(name="stage", bufs=4))
+        psum = ctx.enter_context(tc.psum_pool(name="psum", bufs=8))
+        ctx.enter_context(tc.manual_schedule())
+
+        ident = keep.tile([P, P], F32, name="ident")
+        perm = keep.tile([P, P], F32, name="perm")
+        select = keep.tile([P, 2, P], BF16, name="select")
+        f_rows = keep.tile([P, 3, 2 * GROUP], BF16, name="f_rows")
+        cos = keep.tile([P, 2, 3, 2, GROUP], F32, name="cos")
+        sin = keep.tile([P, 2, 3, 2, GROUP], F32, name="sin")
+        x_rows = [keep.tile([P, DIM], BF16, name="x_rows%d" % j, align_bytes=64) for j in range(TILES)]
+        x_t = [[keep.tile([P, 4 * P], BF16, name="x_t%d_%d" % (j, g), align_bytes=64) for g in range(PASSES)] for j in range(TILES)]
+        x_codes = [[keep.tile([P, P], U32, name="x_codes%d_%d" % (j, g), align_bytes=64) for g in range(PASSES)] for j in range(TILES)]
+        x_scales = [[keep.tile([P, P], U8, name="x_scales%d_%d" % (j, g), align_bytes=64) for g in range(PASSES)] for j in range(TILES)]
+        w_tiles = [keep.tile([P, PASSES, 2 * (c1 - c0)], U8, name="w%d" % c0, align_bytes=64) for c0, c1 in W_CHUNKS]
+        s_tiles = [keep.tile([P, PASSES, c1 - c0], U8, name="s%d" % c0, align_bytes=64) for c0, c1 in S_CHUNKS]
+        v_tiles = [keep.tile([P, h1 - h0, TILES, DH], F32, name="v%d" % h0) for h0, h1 in V_STORES]
+
+        def load_x(j):
+            nc.sync.dma_start(out=x_rows[j][:], in_=x.rearrange("b (q j) k -> (b q) j k", j=TILES)[:, j, :])
+
+        def load_w(i):
+            c0, c1 = W_CHUNKS[i]
+            nc.sync.dma_start(
+                out=w_tiles[i][:].bitcast(I32),
+                in_=w_words[:, :, 2 * c0 : 2 * c1].rearrange("g p n -> p g n").bitcast(I32),
+            )
+
+        def load_scales(i):
+            c0, c1 = S_CHUNKS[i]
+            for r in range(4):
+                nc.sync.dma_start(
+                    out=s_tiles[i][r:P:32, :, :].bitcast(I32),
+                    in_=w_scales[:, r:16:4, c0:c1].rearrange("g r n -> r g n").bitcast(I32),
+                )
+
+        def w_operand(g, c0, c1):
+            for (w0, w1), w in zip(W_CHUNKS, w_tiles):
+                if w0 <= c0 < w1:
+                    codes = w[:, g, 2 * (c0 - w0) : 2 * (c1 - w0)].bitcast(E2M1X4)
+            for (s0, s1), s in zip(S_CHUNKS, s_tiles):
+                if s0 <= c0 < s1:
+                    scales = s[:, g, c0 - s0 : c1 - s0]
+            return codes, scales
+
+        def transpose_x(j):
+            words = x_rows[j][:].bitcast(F32)
+            banks = []
+            for g in range(PASSES):
+                bank = psum.tile([P, 512], F32, name="bank")
+                for u in range(2):
+                    nc.tensor.transpose(bank[:, P * u : P * (u + 1)], words[:, 256 * g + u : 256 * (g + 1) : 2], perm[:])
+                banks.append(bank)
+            return banks
+
+        def interleave(copy, j, g, bank):
+            copy(out=x_t[j][g][:].bitcast(F32), in_=bank[:, : 2 * P].rearrange("p (u m) -> p m u", u=2))
+
+        def quantize(j, g):
+            nc.vector.quantize_mx(out=x_codes[j][g][:].bitcast(E5M2X4), scales=x_scales[j][g][:], in_=x_t[j][g][:])
+
+        def project(j, c0, widths):
+            bank = psum.tile([P, 512], F32, name="bank")
+            at = 0
+            for n in widths:
+                for g in range(PASSES):
+                    codes, scales = w_operand(g, c0 + at, c0 + at + n)
+                    nc.tensor.matmul_mx(
+                        out=bank[:, at : at + n],
+                        lhsT=x_codes[j][g][:].bitcast(E5M2X4),
+                        lhsT_scale=x_scales[j][g][:],
+                        rhs=codes,
+                        rhs_scale=scales,
+                        start=(g == 0),
+                        stop=(g == PASSES - 1),
+                    )
+                at += n
+            return bank
+
+        def products(j, bank, terms):
+            t = bank[:, :ROPE_COLS]
+            nc.vector.tensor_tensor(
+                out=terms[:, 0, j % 2, :],
+                in0=t,
+                in1=cos[:, j // 2 : j // 2 + 1, :, j % 2, :].to_broadcast([P, ROPE_HEADS, 3, GROUP]),
+                op=MULT,
+            )
+            nc.vector.tensor_tensor(
+                out=terms[:, 1, j % 2, :],
+                in0=t.rearrange("p (a s i) -> p a s i", s=2, i=HALF)[:, :, ::-1, :],
+                in1=sin[:, j // 2 : j // 2 + 1, :, j % 2, :].to_broadcast([P, ROPE_HEADS, 3, GROUP]),
+                op=MULT,
+            )
+
+        def add_terms(engine, pair, terms, rotated):
+            engine.tensor_tensor(
+                out=rotated[:, :, 2 * pair : 2 * pair + 2, :],
+                in0=terms[:, 0, :, :].rearrange("p j (h d) -> p h j d", d=DH),
+                in1=terms[:, 1, :, :].rearrange("p j (h d) -> p h j d", d=DH),
+                op=ADD,
+            )
+
+        def store(dst, h0, h1, src):
+            for b in range(B):
+                nc.sync.dma_start(
+                    out=dst[b, h0:h1, :, :].rearrange("h (q j) d -> q h (j d)", j=TILES),
+                    in_=src[b:P:B, :, :, :].rearrange("q h j d -> q h (j d)"),
+                )
+
+        def v_tile(blk, j):
+            c0, c1 = V_BLOCKS[blk]
+            first_whole, last_whole = -(-c0 // DH) * DH, c1 // DH * DH
+            bank = project(j, 2 * WIDTH + c0, (c1 - c0,))
+            for (h0, h1), v in zip(V_STORES, v_tiles):
+                for a0, a1 in ((c0, first_whole), (first_whole, last_whole), (last_whole, c1)):
+                    a0, a1 = max(a0, h0 * DH), min(a1, h1 * DH)
+                    if a0 < a1:
+                        h, d = divmod(a0, DH)
+                        heads = max(1, (a1 - a0) // DH)
+                        wide = (a1 - a0) // heads
+                        nc.scalar.copy(
+                            out=v[:, h - h0 : h - h0 + heads, j, d : d + wide],
+                            in_=bank[:, a0 - c0 : a1 - c0].rearrange("p (h d) -> p h d", h=heads),
+                        )
+            if j == TILES - 1:
+                h0, h1 = V_STORES[blk]
+                store(out_v, h0, h1, v_tiles[blk])
+
+        make_identity(nc, ident[:])
+        nc.vector.memset(s_tiles[0][:].bitcast(I32), 0)
+        nc.vector.tensor_copy(out=perm[:].rearrange("p (q b) -> p q b", b=B), in_=ident[:].rearrange("p (b q) -> p q b", b=B))
+        for half in range(2):
+            nc.vector.tensor_copy(
+                out=select[:, half, :].rearrange("p (q b) -> p q b", b=B),
+                in_=ident[:, half:P:2].unsqueeze(2).to_broadcast([P, P // B, B]),
+            )
+        nc.vector.memset(s_tiles[1][:].bitcast(I32), 0)
+
+        load_x(0)
+        load_w(0)
+        load_scales(0)
+        load_x(1)
+        load_x(2)
+        for a, f in enumerate((f1, f2, f3)):
+            nc.sync.dma_start(out=f_rows[:, a, :], in_=f.rearrange("(r e) d -> r (e d)", e=2))
+        load_x(3)
+        load_w(1)
+        load_scales(1)
+        load_w(2)
+        load_w(3)
+
+        for j in range(2):
+            banks = transpose_x(j)
+            for g in range(PASSES):
+                interleave(nc.vector.tensor_copy, j, g, banks[g])
+                if g > 0:
+                    quantize(j, g - 1)
+            quantize(j, PASSES - 1)
+        banks = transpose_x(2)
+        angles = psum.tile([P, 512], F32, name="bank")
+        for half in range(2):
+            nc.tensor.matmul(
+                out=angles[:, 192 * half : 192 * (half + 1)],
+                lhsT=select[:, half, :],
+                rhs=f_rows[:].rearrange("p a d -> p (a d)"),
+                start=True,
+                stop=True,
+            )
+        angle_groups = angles[:, :384].rearrange("p (a d) -> p a d", d=GROUP)
+        sin_groups = sin[:].rearrange("p j a e d -> p (j a e) d")
+        nc.scalar.activation(out=cos[:].rearrange("p j a e d -> p (j a e d)"), in_=angles[:, :384], func=SIN, scale=-1.0, bias=math.pi / 2)
+        nc.scalar.activation(out=sin_groups[:, :, :HALF], in_=angle_groups[:, :, :HALF], func=SIN, scale=-1.0)
+        nc.scalar.activation(out=sin_groups[:, :, HALF:], in_=angle_groups[:, :, HALF:], func=SIN, scale=1.0)
+
+        for g in range(PASSES):
+            interleave(nc.scalar.copy, 2, g, banks[g])
+            quantize(2, g)
+
+        v_done = 0
+        for blk in range(ROPE_BLOCKS):
+            rotated = stage.tile([P, ROPE_HEADS, TILES, DH], F32, name="rotated", bufs=ROPE_BLOCKS)
+            for pair in range(2):
+                terms = stage.tile([P, 2, 2, ROPE_COLS], F32, name="terms")
+                for j in (2 * pair, 2 * pair + 1):
+                    bank = project(j, ROPE_COLS * blk, (256, 128))
+                    if blk == 0 and j == 0:
+                        banks = transpose_x(TILES - 1)
+                        for g in range(PASSES):
+                            interleave(nc.scalar.copy, TILES - 1, g, banks[g])
+                    products(j, bank, terms)
+                    if blk == 0 and j == 0:
+                        for g in range(PASSES):
+                            quantize(TILES - 1, g)
+                    if blk >= 3 and j % 2 == 1 and v_done < 2 * TILES:
+                        v_tile(v_done // TILES, v_done % TILES)
+                        v_done += 1
+                last = blk == ROPE_BLOCKS - 1 and pair == 1
+                add_terms(nc.vector if last else nc.gpsimd, pair, terms, rotated)
+            h0 = ROPE_HEADS * blk % H
+            store((out_q, out_k)[ROPE_HEADS * blk // H], h0, h0 + ROPE_HEADS, rotated)
+        for blk in (2, 3):
+            for j in range(TILES):
+                v_tile(blk, j)

@@ -30,7 +30,9 @@ ROPE_BLOCKS = 2 * H // ROPE_HEADS
 V_BLOCKS = ((0, 512), (512, 1024), (1024, 1280), (1280, 1536))
 V_STORES = ((0, 5), (5, 10), (10, 13), (13, 16))
 W_CHUNKS = ((0, ROPE_COLS), (ROPE_COLS, WIDTH), (2 * WIDTH, 3 * WIDTH), (WIDTH, 2 * WIDTH))
-S_CHUNKS = ((0, 2 * ROPE_COLS), (2 * ROPE_COLS, 3 * WIDTH))
+S_CHUNKS = ((0, 2 * ROPE_COLS), (2 * ROPE_COLS, WIDTH), (WIDTH, 3 * WIDTH))
+VECTOR_ADDS = (5, 11, 15)
+WEAVE_FROM = 3
 
 
 def tile_attention_pa_kernel(tc, x, f1, f2, f3, w_words, w_scales, out_q, out_k, out_v):
@@ -42,11 +44,9 @@ def tile_attention_pa_kernel(tc, x, f1, f2, f3, w_words, w_scales, out_q, out_k,
         ctx.enter_context(tc.manual_schedule())
 
         ident = keep.tile([P, P], F32, name="ident")
-        perm = keep.tile([P, P], F32, name="perm")
-        select = keep.tile([P, 2, P], BF16, name="select")
-        f_rows = keep.tile([P, 3, 2 * GROUP], BF16, name="f_rows")
-        cos = keep.tile([P, 2, 3, 2, GROUP], F32, name="cos")
-        sin = keep.tile([P, 2, 3, 2, GROUP], F32, name="sin")
+        angles = keep.tile([P, 3, TILES, GROUP], BF16, name="angles")
+        cos = keep.tile([P, TILES, DH], F32, name="cos")
+        sin = keep.tile([P, TILES, DH], F32, name="sin")
         x_rows = [keep.tile([P, DIM], BF16, name="x_rows%d" % j, align_bytes=64) for j in range(TILES)]
         x_t = [[keep.tile([P, 4 * P], BF16, name="x_t%d_%d" % (j, g), align_bytes=64) for g in range(PASSES)] for j in range(TILES)]
         x_codes = [[keep.tile([P, P], U32, name="x_codes%d_%d" % (j, g), align_bytes=64) for g in range(PASSES)] for j in range(TILES)]
@@ -56,7 +56,7 @@ def tile_attention_pa_kernel(tc, x, f1, f2, f3, w_words, w_scales, out_q, out_k,
         v_tiles = [keep.tile([P, h1 - h0, TILES, DH], F32, name="v%d" % h0) for h0, h1 in V_STORES]
 
         def load_x(j):
-            nc.sync.dma_start(out=x_rows[j][:], in_=x.rearrange("b (q j) k -> (b q) j k", j=TILES)[:, j, :])
+            nc.sync.dma_start(out=x_rows[j][:], in_=x.rearrange("b (q j) k -> q b j k", j=TILES)[:, :, j, :])
 
         def load_w(i):
             c0, c1 = W_CHUNKS[i]
@@ -88,7 +88,7 @@ def tile_attention_pa_kernel(tc, x, f1, f2, f3, w_words, w_scales, out_q, out_k,
             for g in range(PASSES):
                 bank = psum.tile([P, 512], F32, name="bank")
                 for u in range(2):
-                    nc.tensor.transpose(bank[:, P * u : P * (u + 1)], words[:, 256 * g + u : 256 * (g + 1) : 2], perm[:])
+                    nc.tensor.transpose(bank[:, P * u : P * (u + 1)], words[:, 256 * g + u : 256 * (g + 1) : 2], ident[:])
                 banks.append(bank)
             return banks
 
@@ -121,13 +121,13 @@ def tile_attention_pa_kernel(tc, x, f1, f2, f3, w_words, w_scales, out_q, out_k,
             nc.vector.tensor_tensor(
                 out=terms[:, 0, j % 2, :],
                 in0=t,
-                in1=cos[:, j // 2 : j // 2 + 1, :, j % 2, :].to_broadcast([P, ROPE_HEADS, 3, GROUP]),
+                in1=cos[:, j : j + 1, :].to_broadcast([P, ROPE_HEADS, DH]),
                 op=MULT,
             )
             nc.vector.tensor_tensor(
                 out=terms[:, 1, j % 2, :],
                 in0=t.rearrange("p (a s i) -> p a s i", s=2, i=HALF)[:, :, ::-1, :],
-                in1=sin[:, j // 2 : j // 2 + 1, :, j % 2, :].to_broadcast([P, ROPE_HEADS, 3, GROUP]),
+                in1=sin[:, j : j + 1, :].to_broadcast([P, ROPE_HEADS, DH]),
                 op=MULT,
             )
 
@@ -140,10 +140,10 @@ def tile_attention_pa_kernel(tc, x, f1, f2, f3, w_words, w_scales, out_q, out_k,
             )
 
         def store(dst, h0, h1, src):
-            for b in range(B):
+            for h in range(h0, h1):
                 nc.sync.dma_start(
-                    out=dst[b, h0:h1, :, :].rearrange("h (q j) d -> q h (j d)", j=TILES),
-                    in_=src[b:P:B, :, :, :].rearrange("q h j d -> q h (j d)"),
+                    out=dst[:, h, :, :].rearrange("b (q j) d -> q b (j d)", j=TILES),
+                    in_=src[:, h - h0, :, :].rearrange("p j d -> p (j d)"),
                 )
 
         def v_tile(blk, j):
@@ -166,77 +166,66 @@ def tile_attention_pa_kernel(tc, x, f1, f2, f3, w_words, w_scales, out_q, out_k,
                 store(out_v, h0, h1, v_tiles[blk])
 
         make_identity(nc, ident[:])
-        nc.vector.memset(s_tiles[0][:].bitcast(I32), 0)
-        nc.vector.tensor_copy(out=perm[:].rearrange("p (q b) -> p q b", b=B), in_=ident[:].rearrange("p (b q) -> p q b", b=B))
-        for half in range(2):
-            nc.vector.tensor_copy(
-                out=select[:, half, :].rearrange("p (q b) -> p q b", b=B),
-                in_=ident[:, half:P:2].unsqueeze(2).to_broadcast([P, P // B, B]),
-            )
-        nc.vector.memset(s_tiles[1][:].bitcast(I32), 0)
+        for s_tile in s_tiles:
+            nc.vector.memset(s_tile[:].bitcast(I32), 0)
 
-        load_x(0)
+        for a, f in enumerate((f1, f2, f3)):
+            nc.sync.dma_start(
+                out=angles[:, a, :, :].rearrange("p j d -> p (j d)"),
+                in_=f.rearrange("(q j) d -> q (j d)", j=TILES).unsqueeze(1).to_broadcast([P // B, B, TILES * GROUP]),
+            )
+        for j in range(TILES):
+            load_x(j)
         load_w(0)
         load_scales(0)
-        load_x(1)
-        load_x(2)
-        for a, f in enumerate((f1, f2, f3)):
-            nc.sync.dma_start(out=f_rows[:, a, :], in_=f.rearrange("(r e) d -> r (e d)", e=2))
-        load_x(3)
         load_w(1)
         load_scales(1)
+        load_scales(2)
         load_w(2)
         load_w(3)
 
-        for j in range(2):
+        by_token = angles[:].rearrange("p a j d -> p j a d")
+        sin_groups = sin[:].rearrange("p j (a d) -> p j a d", d=GROUP)
+        for a in range(3):
+            nc.scalar.activation(
+                out=cos[:, :, GROUP * a : GROUP * (a + 1)], in_=angles[:, a, :, :], func=SIN, scale=-1.0, bias=math.pi / 2
+            )
+        nc.scalar.activation(out=sin_groups[:, :, :, :HALF], in_=by_token[:, :, :, :HALF], func=SIN, scale=-1.0)
+        nc.scalar.activation(out=sin_groups[:, :, :, HALF:], in_=by_token[:, :, :, HALF:], func=SIN, scale=1.0)
+
+        for j in range(TILES):
             banks = transpose_x(j)
             for g in range(PASSES):
-                interleave(nc.vector.tensor_copy, j, g, banks[g])
-                if g > 0:
-                    quantize(j, g - 1)
-            quantize(j, PASSES - 1)
-        banks = transpose_x(2)
-        angles = psum.tile([P, 512], F32, name="bank")
-        for half in range(2):
-            nc.tensor.matmul(
-                out=angles[:, 192 * half : 192 * (half + 1)],
-                lhsT=select[:, half, :],
-                rhs=f_rows[:].rearrange("p a d -> p (a d)"),
-                start=True,
-                stop=True,
-            )
-        angle_groups = angles[:, :384].rearrange("p (a d) -> p a d", d=GROUP)
-        sin_groups = sin[:].rearrange("p j a e d -> p (j a e) d")
-        nc.scalar.activation(out=cos[:].rearrange("p j a e d -> p (j a e d)"), in_=angles[:, :384], func=SIN, scale=-1.0, bias=math.pi / 2)
-        nc.scalar.activation(out=sin_groups[:, :, :HALF], in_=angle_groups[:, :, :HALF], func=SIN, scale=-1.0)
-        nc.scalar.activation(out=sin_groups[:, :, HALF:], in_=angle_groups[:, :, HALF:], func=SIN, scale=1.0)
+                interleave(nc.scalar.copy, j, g, banks[g])
+                quantize(j, g)
 
-        for g in range(PASSES):
-            interleave(nc.scalar.copy, 2, g, banks[g])
-            quantize(2, g)
+        def finish_pair(engine, blk, pair, terms, rotated):
+            add_terms(engine, pair, terms, rotated)
+            if pair == 1:
+                h0 = ROPE_HEADS * blk % H
+                store((out_q, out_k)[ROPE_HEADS * blk // H], h0, h0 + ROPE_HEADS, rotated)
 
         v_done = 0
+        waiting = []
         for blk in range(ROPE_BLOCKS):
             rotated = stage.tile([P, ROPE_HEADS, TILES, DH], F32, name="rotated", bufs=ROPE_BLOCKS)
             for pair in range(2):
                 terms = stage.tile([P, 2, 2, ROPE_COLS], F32, name="terms")
                 for j in (2 * pair, 2 * pair + 1):
                     bank = project(j, ROPE_COLS * blk, (256, 128))
-                    if blk == 0 and j == 0:
-                        banks = transpose_x(TILES - 1)
-                        for g in range(PASSES):
-                            interleave(nc.scalar.copy, TILES - 1, g, banks[g])
                     products(j, bank, terms)
-                    if blk == 0 and j == 0:
-                        for g in range(PASSES):
-                            quantize(TILES - 1, g)
-                    if blk >= 3 and j % 2 == 1 and v_done < 2 * TILES:
+                    if waiting:
+                        finish_pair(nc.vector, *waiting[0])
+                        waiting.clear()
+                    if blk >= WEAVE_FROM and j % 2 == 1 and v_done < 2 * TILES:
                         v_tile(v_done // TILES, v_done % TILES)
                         v_done += 1
-                last = blk == ROPE_BLOCKS - 1 and pair == 1
-                add_terms(nc.vector if last else nc.gpsimd, pair, terms, rotated)
-            h0 = ROPE_HEADS * blk % H
-            store((out_q, out_k)[ROPE_HEADS * blk // H], h0, h0 + ROPE_HEADS, rotated)
-        for blk in (2, 3):
-            for j in range(TILES):
-                v_tile(blk, j)
+                if 2 * blk + pair in VECTOR_ADDS:
+                    waiting.append((blk, pair, terms, rotated))
+                else:
+                    finish_pair(nc.gpsimd, blk, pair, terms, rotated)
+        for j in range(TILES):
+            v_tile(2, j)
+        finish_pair(nc.vector, *waiting[0])
+        for j in range(TILES):
+            v_tile(3, j)

@@ -193,8 +193,16 @@ def tile_attention_pa_kernel(tc, x, f1, f2, f3, w_words, w_scales, out_q, out_k,
         nc.scalar.activation(out=sin_groups[:, :, :, :HALF], in_=by_token[:, :, :, :HALF], func=SIN, scale=-1.0)
         nc.scalar.activation(out=sin_groups[:, :, :, HALF:], in_=by_token[:, :, :, HALF:], func=SIN, scale=1.0)
 
+        def warm_up(count):
+            unread = psum.tile([P, 512], F32, name="bank")
+            for i in range(count):
+                nc.tensor.matmul(out=unread[:, P * i : P * (i + 1)], lhsT=ident[:], rhs=ident[:], start=True, stop=True)
+
+        warm_up(4)
         for j in range(TILES):
             banks = transpose_x(j)
+            if j == 1:
+                warm_up(3)
             for g in range(PASSES):
                 interleave(nc.scalar.copy, j, g, banks[g])
                 quantize(j, g)

import math
from contextlib import ExitStack

import concourse.mybir as mybir
from concourse.masks import make_identity

B, N, DIM, H, DH = 2, 256, 1536, 16, 96
FLOPS = 2 * B * N * DIM * 3 * H * DH

F32 = mybir.dt.float32
BF16 = mybir.dt.bfloat16
I32 = mybir.dt.int32
U32 = mybir.dt.uint32
U8 = mybir.dt.uint8
E5M2X4 = mybir.dt.float8_e5m2_x4
E2M1X4 = mybir.dt.float4_e2m1fn_x4
MULT = mybir.AluOpType.mult
ADD = mybir.AluOpType.add
SIN = mybir.ActivationFunctionType.Sin

P = 128
PASSES = DIM // 512
TILES = 4
WIDTH = H * DH
GROUP = 32
HALF = GROUP // 2
ROPE_HEADS = 4
ROPE_COLS = ROPE_HEADS * DH
ROPE_BLOCKS = 2 * H // ROPE_HEADS
V_BLOCKS = ((0, 512), (512, 1024), (1024, 1280), (1280, 1536))
V_STORES = ((0, 5), (5, 10), (10, 13), (13, 16))
W_CHUNKS = ((0, ROPE_COLS), (ROPE_COLS, WIDTH), (2 * WIDTH, 3 * WIDTH), (WIDTH, 2 * WIDTH))
S_CHUNKS = ((0, 2 * ROPE_COLS), (2 * ROPE_COLS, WIDTH), (WIDTH, 3 * WIDTH))
VECTOR_ADDS = (5, 11, 15)
WEAVE_FROM = 3


def tile_attention_pa_kernel(tc, x, f1, f2, f3, w_words, w_scales, out_q, out_k, out_v):
    nc = tc.nc
    with ExitStack() as ctx:
        keep = ctx.enter_context(tc.tile_pool(name="keep", bufs=1))
        stage = ctx.enter_context(tc.tile_pool(name="stage", bufs=4))
        psum = ctx.enter_context(tc.psum_pool(name="psum", bufs=8))
        ctx.enter_context(tc.manual_schedule())

        ident = keep.tile([P, P], F32, name="ident")
        angles = keep.tile([P, 3, TILES, GROUP], BF16, name="angles")
        cos = keep.tile([P, TILES, DH], F32, name="cos")
        sin = keep.tile([P, TILES, DH], F32, name="sin")
        x_rows = [keep.tile([P, DIM], BF16, name="x_rows%d" % j, align_bytes=64) for j in range(TILES)]
        x_t = [[keep.tile([P, 4 * P], BF16, name="x_t%d_%d" % (j, g), align_bytes=64) for g in range(PASSES)] for j in range(TILES)]
        x_codes = [[keep.tile([P, P], U32, name="x_codes%d_%d" % (j, g), align_bytes=64) for g in range(PASSES)] for j in range(TILES)]
        x_scales = [[keep.tile([P, P], U8, name="x_scales%d_%d" % (j, g), align_bytes=64) for g in range(PASSES)] for j in range(TILES)]
        w_tiles = [keep.tile([P, PASSES, 2 * (c1 - c0)], U8, name="w%d" % c0, align_bytes=64) for c0, c1 in W_CHUNKS]
        s_tiles = [keep.tile([P, PASSES, c1 - c0], U8, name="s%d" % c0, align_bytes=64) for c0, c1 in S_CHUNKS]
        v_tiles = [keep.tile([P, h1 - h0, TILES, DH], F32, name="v%d" % h0) for h0, h1 in V_STORES]

        def load_x(j):
            nc.sync.dma_start(out=x_rows[j][:], in_=x.rearrange("b (q j) k -> q b j k", j=TILES)[:, :, j, :])

        def load_w(i):
            c0, c1 = W_CHUNKS[i]
            nc.sync.dma_start(
                out=w_tiles[i][:].bitcast(I32),
                in_=w_words[:, :, 2 * c0 : 2 * c1].rearrange("g p n -> p g n").bitcast(I32),
            )

        def load_scales(i):
            c0, c1 = S_CHUNKS[i]
            for r in range(4):
                nc.sync.dma_start(
                    out=s_tiles[i][r:P:32, :, :].bitcast(I32),
                    in_=w_scales[:, r:16:4, c0:c1].rearrange("g r n -> r g n").bitcast(I32),
                )

        def w_operand(g, c0, c1):
            for (w0, w1), w in zip(W_CHUNKS, w_tiles):
                if w0 <= c0 < w1:
                    codes = w[:, g, 2 * (c0 - w0) : 2 * (c1 - w0)].bitcast(E2M1X4)
            for (s0, s1), s in zip(S_CHUNKS, s_tiles):
                if s0 <= c0 < s1:
                    scales = s[:, g, c0 - s0 : c1 - s0]
            return codes, scales

        def transpose_x(j):
            words = x_rows[j][:].bitcast(F32)
            banks = []
            for g in range(PASSES):
                bank = psum.tile([P, 512], F32, name="bank")
                for u in range(2):
                    nc.tensor.transpose(bank[:, P * u : P * (u + 1)], words[:, 256 * g + u : 256 * (g + 1) : 2], ident[:])
                banks.append(bank)
            return banks

        def interleave(copy, j, g, bank):
            copy(out=x_t[j][g][:].bitcast(F32), in_=bank[:, : 2 * P].rearrange("p (u m) -> p m u", u=2))

        def quantize(j, g):
            nc.vector.quantize_mx(out=x_codes[j][g][:].bitcast(E5M2X4), scales=x_scales[j][g][:], in_=x_t[j][g][:])

        def project(j, c0, widths):
            bank = psum.tile([P, 512], F32, name="bank")
            at = 0
            for n in widths:
                for g in range(PASSES):
                    codes, scales = w_operand(g, c0 + at, c0 + at + n)
                    nc.tensor.matmul_mx(
                        out=bank[:, at : at + n],
                        lhsT=x_codes[j][g][:].bitcast(E5M2X4),
                        lhsT_scale=x_scales[j][g][:],
                        rhs=codes,
                        rhs_scale=scales,
                        start=(g == 0),
                        stop=(g == PASSES - 1),
                    )
                at += n
            return bank

        def products(j, bank, terms):
            t = bank[:, :ROPE_COLS]
            nc.vector.tensor_tensor(
                out=terms[:, 0, j % 2, :],
                in0=t,
                in1=cos[:, j : j + 1, :].to_broadcast([P, ROPE_HEADS, DH]),
                op=MULT,
            )
            nc.vector.tensor_tensor(
                out=terms[:, 1, j % 2, :],
                in0=t.rearrange("p (a s i) -> p a s i", s=2, i=HALF)[:, :, ::-1, :],
                in1=sin[:, j : j + 1, :].to_broadcast([P, ROPE_HEADS, DH]),
                op=MULT,
            )

        def add_terms(engine, pair, terms, rotated):
            engine.tensor_tensor(
                out=rotated[:, :, 2 * pair : 2 * pair + 2, :],
                in0=terms[:, 0, :, :].rearrange("p j (h d) -> p h j d", d=DH),
                in1=terms[:, 1, :, :].rearrange("p j (h d) -> p h j d", d=DH),
                op=ADD,
            )

        def store(dst, h0, h1, src):
            for h in range(h0, h1):
                nc.sync.dma_start(
                    out=dst[:, h, :, :].rearrange("b (q j) d -> q b (j d)", j=TILES),
                    in_=src[:, h - h0, :, :].rearrange("p j d -> p (j d)"),
                )

        def v_tile(blk, j):
            c0, c1 = V_BLOCKS[blk]
            first_whole, last_whole = -(-c0 // DH) * DH, c1 // DH * DH
            bank = project(j, 2 * WIDTH + c0, (c1 - c0,))
            for (h0, h1), v in zip(V_STORES, v_tiles):
                for a0, a1 in ((c0, first_whole), (first_whole, last_whole), (last_whole, c1)):
                    a0, a1 = max(a0, h0 * DH), min(a1, h1 * DH)
                    if a0 < a1:
                        h, d = divmod(a0, DH)
                        heads = max(1, (a1 - a0) // DH)
                        wide = (a1 - a0) // heads
                        nc.scalar.copy(
                            out=v[:, h - h0 : h - h0 + heads, j, d : d + wide],
                            in_=bank[:, a0 - c0 : a1 - c0].rearrange("p (h d) -> p h d", h=heads),
                        )
            if j == TILES - 1:
                h0, h1 = V_STORES[blk]
                store(out_v, h0, h1, v_tiles[blk])

        make_identity(nc, ident[:])
        for s_tile in s_tiles:
            nc.vector.memset(s_tile[:].bitcast(I32), 0)

        for a, f in enumerate((f1, f2, f3)):
            nc.sync.dma_start(
                out=angles[:, a, :, :].rearrange("p j d -> p (j d)"),
                in_=f.rearrange("(q j) d -> q (j d)", j=TILES).unsqueeze(1).to_broadcast([P // B, B, TILES * GROUP]),
            )
        for j in range(TILES):
            load_x(j)
        load_w(0)
        load_scales(0)
        load_w(1)
        load_scales(1)
        load_scales(2)
        load_w(2)
        load_w(3)

        by_token = angles[:].rearrange("p a j d -> p j a d")
        sin_groups = sin[:].rearrange("p j (a d) -> p j a d", d=GROUP)
        for a in range(3):
            nc.scalar.activation(
                out=cos[:, :, GROUP * a : GROUP * (a + 1)], in_=angles[:, a, :, :], func=SIN, scale=-1.0, bias=math.pi / 2
            )
        nc.scalar.activation(out=sin_groups[:, :, :, :HALF], in_=by_token[:, :, :, :HALF], func=SIN, scale=-1.0)
        nc.scalar.activation(out=sin_groups[:, :, :, HALF:], in_=by_token[:, :, :, HALF:], func=SIN, scale=1.0)

        def warm_up(count):
            unread = psum.tile([P, 512], F32, name="bank")
            for i in range(count):
                nc.tensor.matmul(out=unread[:, P * i : P * (i + 1)], lhsT=ident[:], rhs=ident[:], start=True, stop=True)

        warm_up(4)
        for j in range(TILES):
            banks = transpose_x(j)
            if j == 1:
                warm_up(3)
            for g in range(PASSES):
                interleave(nc.scalar.copy, j, g, banks[g])
                quantize(j, g)

        def finish_pair(engine, blk, pair, terms, rotated):
            add_terms(engine, pair, terms, rotated)
            if pair == 1:
                h0 = ROPE_HEADS * blk % H
                store((out_q, out_k)[ROPE_HEADS * blk // H], h0, h0 + ROPE_HEADS, rotated)

        v_done = 0
        waiting = []
        for blk in range(ROPE_BLOCKS):
            rotated = stage.tile([P, ROPE_HEADS, TILES, DH], F32, name="rotated", bufs=ROPE_BLOCKS)
            for pair in range(2):
                terms = stage.tile([P, 2, 2, ROPE_COLS], F32, name="terms")
                for j in (2 * pair, 2 * pair + 1):
                    bank = project(j, ROPE_COLS * blk, (256, 128))
                    products(j, bank, terms)
                    if waiting:
                        finish_pair(nc.vector, *waiting[0])
                        waiting.clear()
                    if blk >= WEAVE_FROM and j % 2 == 1 and v_done < 2 * TILES:
                        v_tile(v_done // TILES, v_done % TILES)
                        v_done += 1
                if 2 * blk + pair in VECTOR_ADDS:
                    waiting.append((blk, pair, terms, rotated))
                else:
                    finish_pair(nc.gpsimd, blk, pair, terms, rotated)
        for j in range(TILES):
            v_tile(2, j)
        finish_pair(nc.vector, *waiting[0])
        for j in range(TILES):
            v_tile(3, j)
